import numpy as np
import ml_dtypes


def mxq(x, axis, fmt="e4m3"):
    dtype, down = {"e4m3": (ml_dtypes.float8_e4m3fn, 7), "e5m2": (ml_dtypes.float8_e5m2, 14)}[fmt]
    v = np.moveaxis(np.asarray(x, np.float32).astype(ml_dtypes.bfloat16).astype(np.float64), axis, -1)
    blocks = v.reshape(v.shape[:-1] + (-1, 32))
    amax = np.abs(blocks).max(-1, keepdims=True)
    byte = np.maximum(np.where(amax > 0, np.frexp(amax)[1] - 1 + 127, 0) - down, 1)
    scale = np.exp2(byte - 127.0)
    codes = (blocks / scale).astype(np.float32).astype(dtype).astype(np.float64)
    return np.moveaxis((codes * scale).reshape(v.shape), -1, axis)


WIDE = False


def mx_kscale(k):
    if not WIDE:
        return np.ones(k)
    levels = np.array([10, -10, 5, -5, 0])
    a = np.random.permutation(np.resize(levels, k // 512 * 4)).reshape(k // 512, 4)
    idx = np.arange(k)
    return np.exp2(a[idx // 512, idx % 128 // 32])


BF16 = ml_dtypes.bfloat16


def bf(x):
    return np.asarray(x, np.float32).astype(BF16)


def f64(x):
    return np.asarray(x).astype(np.float64)


E2M1 = np.array([0.0, 0.5, 1.0, 1.5, 2.0, 3.0, 4.0, 6.0, -0.0, -0.5, -1.0, -1.5, -2.0, -3.0, -4.0, -6.0])


def pack_weight(w, fmt):
    k, n = w.shape
    w = f64(bf(w)).reshape(k // 32, 32, n)
    amax = np.abs(w).max(1)
    if fmt == "e4m3":
        byte = np.frexp(amax)[1] - 1 + 127 - 7
    else:
        mant, ex = np.frexp(amax / 6.0)
        byte = np.where(mant > 0.5, ex, ex - 1) + 127
    byte = np.clip(np.where(amax > 0, byte, 1), 1, 254)
    scaled = (w * np.exp2(127.0 - byte)[:, None, :]).reshape(k, n).astype(np.float32)
    by_word = np.ascontiguousarray(scaled.reshape(k // 512, 128, 4, n).transpose(0, 1, 3, 2))
    if fmt == "e4m3":
        words = by_word.astype(ml_dtypes.float8_e4m3fn).view(np.uint8)
    else:
        c = by_word.astype(ml_dtypes.float4_e2m1fn).view(np.uint8) & 0xF
        words = c[..., 0::2] | (c[..., 1::2] << 4)
    return np.ascontiguousarray(words), np.ascontiguousarray(byte.astype(np.uint8).reshape(k // 512, 16, n))


def unpack_weight(words, scales, fmt):
    g, p, n, _ = words.shape
    if fmt == "e4m3":
        vals = np.ascontiguousarray(words).view(ml_dtypes.float8_e4m3fn).astype(np.float64)
    else:
        nib = np.empty((g, p, n, 4), np.uint8)
        nib[..., 0::2] = words & 0xF
        nib[..., 1::2] = words >> 4
        vals = E2M1[nib]
    vals = vals * np.repeat(np.exp2(scales.astype(np.float64) - 127.0), 8, axis=1)[..., None]
    return vals.transpose(0, 1, 3, 2).reshape(g * 512, n)


B, IN_CH, OUT_CH, KH, KW, H, W_IN = 2, 64, 1024, 4, 4, 11, 11
HO, WO = H - KH + 1, W_IN - KW + 1
L = HO * WO
KD = KH * KW
F = IN_CH * KD * KD
MXB = 32
FMT = "e4m3"


def setup_inputs():
    s = mx_kscale(F)[(np.arange(IN_CH) * KD * KD) // MXB * MXB]
    u = np.exp2(np.round(np.log2(s) / 2))
    x = bf(np.random.standard_normal((B, IN_CH, H, W_IN)) * u[None, :, None, None])
    w = np.random.standard_normal((OUT_CH, F)) / np.sqrt(F) / np.repeat(u * u, KD * KD)[None, :]
    words, scales = pack_weight(np.ascontiguousarray(w.T), FMT)
    return {"x": x, "W_words": words, "W_scales": scales}


def _unfold(x):
    patches = np.stack([x[:, :, i:i + HO, j:j + WO] for i in range(KH) for j in range(KW)], axis=2)
    return patches.reshape(B, IN_CH, KD, L).transpose(0, 3, 1, 2)


def reference(x, W_words, W_scales):
    p = _unfold(f64(x))
    outer = np.einsum("blci,blcj->blcij", p, p)
    feat = outer.reshape(B, L, F)
    out = unpack_weight(W_words, W_scales, FMT).T @ mxq(feat, 2, "e4m3").transpose(0, 2, 1)
    return out.reshape(B, OUT_CH, HO, WO)

@@ -1,0 +1,181 @@
+from contextlib import ExitStack
+
+import concourse.mybir as mybir
+from concourse.masks import make_identity
+
+BF16 = mybir.dt.bfloat16
+F32 = mybir.dt.float32
+I32 = mybir.dt.int32
+U32 = mybir.dt.uint32
+U8 = mybir.dt.uint8
+FP8X4 = mybir.dt.float8_e4m3fn_x4
+
+P = 128
+IMAGES, CHANNELS, SIDE = 2, 64, 11
+GRID = 8
+POSITIONS = IMAGES * GRID * GRID
+TAPS = 16
+OUT_CH = 1024
+K_PASS = 512
+GROUPS = CHANNELS * TAPS * TAPS // K_PASS
+CHUNK = 4
+CHUNKS = GROUPS // CHUNK
+CHUNK_CH = 2 * CHUNK
+N_TILE = 512
+LEAD = 1
+
+FLOPS = 2 * POSITIONS * CHANNELS * TAPS * TAPS * OUT_CH
+
+
+def tile_fast2order_de_conv_k_kernel(tc, x, W_words, W_scales, out):
+    nc = tc.nc
+    with ExitStack() as ctx:
+        const = ctx.enter_context(tc.tile_pool(name="const", bufs=1))
+        weights = ctx.enter_context(tc.tile_pool(name="weights", bufs=1))
+        codes_pool = ctx.enter_context(tc.tile_pool(name="codes", bufs=1))
+        feat_pool = ctx.enter_context(tc.tile_pool(name="feat", bufs=3))
+        grouped_pool = ctx.enter_context(tc.tile_pool(name="grouped", bufs=3))
+        acc_pool = ctx.enter_context(tc.psum_pool(name="acc", bufs=1))
+        turn_pool = ctx.enter_context(tc.psum_pool(name="turn", bufs=6))
+        ctx.enter_context(tc.manual_schedule())
+
+        xs = const.tile([P, IMAGES, SIDE * SIDE], BF16)
+        x_by_channel = x.rearrange("n c h w -> c n (h w)")
+        run = SIDE * SIDE - 1
+        for h in range(2):
+            nc.sync.dma_start(
+                out=xs[CHANNELS * h : CHANNELS * (h + 1), :, 0:run],
+                in_=x_by_channel[:, :, h : h + run],
+            )
+
+        w_planes = []
+        w_words = []
+        for quad in range(GROUPS // 4):
+            planes = weights.tile([P, OUT_CH], U8, name="planes%d" % quad, align_bytes=64)
+            nc.vector.memset(planes[:].bitcast(I32), 0)
+            w_planes.append(planes)
+        for quad in range(GROUPS // 4):
+            for q in range(4):
+                nc.sync.dma_start(
+                    out=w_planes[quad][32 * q : 32 * q + 16, :].bitcast(I32),
+                    in_=W_scales[4 * quad : 4 * quad + 4, 4 * q : 4 * q + 4, :].bitcast(I32),
+                )
+            for g in range(4 * quad, 4 * quad + 4):
+                words = weights.tile([P, OUT_CH], U32, name="words%d" % g, align_bytes=64)
+                nc.sync.dma_start(
+                    out=words[:].bitcast(I32),
+                    in_=W_words[g].rearrange("p n t -> p (n t)").bitcast(I32),
+                )
+                w_words.append(words)
+
+        ident_bf = const.tile([P, P], BF16)
+        make_identity(nc, ident_bf[:])
+        ident_f32 = const.tile([P, P], F32)
+        make_identity(nc, ident_f32[:])
+
+        rows = xs[:].rearrange("p n (r w) -> p n r w", w=SIDE)
+        windows = const.tile([P, TAPS // 2, IMAGES, GRID, GRID], BF16)
+        for s in range(TAPS // 2):
+            a, b_hi = divmod(s, 2)
+            window = rows[:, :, a : a + GRID, 2 * b_hi : 2 * b_hi + GRID]
+            if s % 2 == 0:
+                nc.vector.tensor_copy(out=windows[:, s], in_=window)
+            else:
+                nc.scalar.copy(out=windows[:, s], in_=window)
+        by_tap = turn_pool.tile([P, TAPS, CHANNELS], BF16, tag="turn")
+        for s in range(TAPS // 2):
+            nc.tensor.transpose(
+                by_tap[:, 2 * s : 2 * s + 2, :].rearrange("p h c -> p (h c)"),
+                windows[:, s].rearrange("p n y z -> p (n y z)"),
+                ident_bf[:],
+            )
+        patches = const.tile([P, CHANNELS, TAPS], BF16)
+        nc.vector.tensor_copy(out=patches[:], in_=by_tap[:].rearrange("p i c -> p c i"))
+        halves = const.tile([P, 2, CHANNELS, TAPS // 2], BF16)
+        nc.vector.tensor_copy(
+            out=halves[:].bitcast(F32),
+            in_=patches[:].bitcast(F32).rearrange("p c (jh u) -> p u c jh", u=2),
+        )
+
+        acc = [
+            acc_pool.tile([P, N_TILE], F32, name="acc%d" % half) for half in range(OUT_CH // N_TILE)
+        ]
+        grouped_of = {}
+
+        def multiply_and_turn(chunk):
+            c0 = CHUNK_CH * chunk
+            shape = [P, CHUNK_CH, TAPS, TAPS // 2]
+            feat = feat_pool.tile([P, 2, CHUNK_CH, TAPS, TAPS // 2], BF16)
+            first = patches[:, c0 : c0 + CHUNK_CH, :].unsqueeze(3).to_broadcast(shape)
+            for u in range(2):
+                second = halves[:, u, c0 : c0 + CHUNK_CH, :].unsqueeze(2).to_broadcast(shape)
+                nc.vector.tensor_mul(out=feat[:, u], in0=first, in1=second)
+            feat_words = feat[:].rearrange("p u c i k -> p (u c i k)").bitcast(F32)
+            grouped = grouped_pool.tile([P, CHUNK, POSITIONS, 4], BF16, align_bytes=64)
+            grouped_words = grouped[:].bitcast(F32)
+            for pair in range(CHUNK // 2):
+                turned = turn_pool.tile([P, 2, 2, POSITIONS], F32, tag="turn")
+                for g_in_pair in range(2):
+                    for u in range(2):
+                        start = (CHUNK * u + 2 * pair + g_in_pair) * P
+                        nc.tensor.transpose(
+                            turned[:, g_in_pair, u, :],
+                            feat_words[:, start : start + P],
+                            ident_f32[:],
+                        )
+                nc.scalar.copy(
+                    out=grouped_words[:, 2 * pair : 2 * pair + 2],
+                    in_=turned[:].rearrange("p g u r -> p g r u"),
+                )
+            grouped_of[chunk] = grouped
+
+        def quantise_and_contract(chunk):
+            codes = codes_pool.tile([P, CHUNK * POSITIONS], U32, name="codes%d" % chunk, align_bytes=64)
+            scales = codes_pool.tile([P, CHUNK * POSITIONS], U8, name="scales%d" % chunk, align_bytes=64)
+            nc.vector.quantize_mx(
+                out=codes[:].bitcast(FP8X4),
+                scales=scales[:],
+                in_=grouped_of[chunk][:].rearrange("p g r t -> p (g r t)"),
+            )
+            for g_in_chunk in range(CHUNK):
+                g = CHUNK * chunk + g_in_chunk
+                cols = slice(POSITIONS * g_in_chunk, POSITIONS * (g_in_chunk + 1))
+                for half in range(OUT_CH // N_TILE):
+                    n_cols = slice(N_TILE * half, N_TILE * (half + 1))
+                    nc.tensor.matmul_mx(
+                        out=acc[half][:],
+                        lhsT=codes[:, cols].bitcast(FP8X4),
+                        lhsT_scale=scales[:, cols],
+                        rhs=w_words[g][:, n_cols].bitcast(FP8X4),
+                        rhs_scale=w_planes[g // 4][4 * (g % 4) : P, n_cols],
+                        start=(g == 0),
+                        stop=(g == GROUPS - 1),
+                    )
+
+        for step in range(CHUNKS + LEAD):
+            if step < CHUNKS:
+                multiply_and_turn(step)
+            if step >= LEAD:
+                quantise_and_contract(step - LEAD)
+
+        by_position = const.tile([P, OUT_CH], F32)
+        nc.vector.tensor_copy(out=by_position[:, 0:N_TILE], in_=acc[0][:])
+        nc.scalar.copy(out=by_position[:, N_TILE : 2 * N_TILE], in_=acc[1][:])
+        by_channel = const.tile([P, OUT_CH // P, POSITIONS], F32)
+        out_view = out.rearrange("n (t p) y z -> p t n (y z)", p=P)
+        per_bank = N_TILE // P
+        for half in range(OUT_CH // N_TILE):
+            turned_out = turn_pool.tile([P, per_bank, POSITIONS], F32, tag="turn")
+            for t in range(per_bank):
+                o0 = N_TILE * half + P * t
+                nc.tensor.transpose(turned_out[:, t, :], by_position[:, o0 : o0 + P], ident_f32[:])
+            tiles = slice(per_bank * half, per_bank * (half + 1))
+            if half == 0:
+                nc.vector.tensor_copy(out=by_channel[:, tiles, :], in_=turned_out[:])
+            else:
+                nc.scalar.copy(out=by_channel[:, tiles, :], in_=turned_out[:])
+            for n in range(IMAGES):
+                nc.sync.dma_start(
+                    out=out_view[:, tiles, n, :],
+                    in_=by_channel[:, tiles, GRID * GRID * n : GRID * GRID * (n + 1)],
+                )

@@ -54,12 +54,17 @@ def tile_fast2order_de_conv_k_kernel(tc, x, W_words, W_scales, out):
             planes = weights.tile([P, OUT_CH], U8, name="planes%d" % quad, align_bytes=64)
             nc.vector.memset(planes[:].bitcast(I32), 0)
             w_planes.append(planes)
+        ident_bf = const.tile([P, P], BF16)
+        make_identity(nc, ident_bf[:])
+        ident_f32 = const.tile([P, P], F32)
         for quad in range(GROUPS // 4):
             for q in range(4):
-                nc.sync.dma_start(
-                    out=w_planes[quad][32 * q : 32 * q + 16, :].bitcast(I32),
-                    in_=W_scales[4 * quad : 4 * quad + 4, 4 * q : 4 * q + 4, :].bitcast(I32),
+                nc.gpsimd.dma_start(
+                    out=w_planes[quad][32 * q : 32 * q + 16, :].bitcast(F32),
+                    in_=W_scales[4 * quad : 4 * quad + 4, 4 * q : 4 * q + 4, :].bitcast(F32),
                 )
+            if quad == 0:
+                make_identity(nc, ident_f32[:])
             for g in range(4 * quad, 4 * quad + 4):
                 words = weights.tile([P, OUT_CH], U32, name="words%d" % g, align_bytes=64)
                 nc.sync.dma_start(
@@ -67,11 +72,6 @@ def tile_fast2order_de_conv_k_kernel(tc, x, W_words, W_scales, out):
                     in_=W_words[g].rearrange("p n t -> p (n t)").bitcast(I32),
                 )
                 w_words.append(words)
-
-        ident_bf = const.tile([P, P], BF16)
-        make_identity(nc, ident_bf[:])
-        ident_f32 = const.tile([P, P], F32)
-        make_identity(nc, ident_f32[:])
 
         rows = xs[:].rearrange("p n (r w) -> p n r w", w=SIDE)
         windows = const.tile([P, TAPS // 2, IMAGES, GRID, GRID], BF16)

@@ -22,7 +22,10 @@ CHUNK = 4
 CHUNKS = GROUPS // CHUNK
 CHUNK_CH = 2 * CHUNK
 N_TILE = 512
+HALVES = OUT_CH // N_TILE
 LEAD = 1
+FIRST_SPLIT = GROUPS - 2
+PER_ROW = N_TILE // P
 
 FLOPS = 2 * POSITIONS * CHANNELS * TAPS * TAPS * OUT_CH
 
@@ -43,13 +46,13 @@ def tile_fast2order_de_conv_k_kernel(tc, x, W_words, W_scales, out):
         x_by_channel = x.rearrange("n c h w -> c n (h w)")
         run = SIDE * SIDE - 1
         for h in range(2):
-            nc.sync.dma_start(
+            nc.scalar.dma_start(
                 out=xs[CHANNELS * h : CHANNELS * (h + 1), :, 0:run],
                 in_=x_by_channel[:, :, h : h + run],
             )
 
         w_planes = []
-        w_words = []
+        w_cols = {}
         for quad in range(GROUPS // 4):
             planes = weights.tile([P, OUT_CH], U8, name="planes%d" % quad, align_bytes=64)
             nc.vector.memset(planes[:].bitcast(I32), 0)
@@ -65,13 +68,24 @@ def tile_fast2order_de_conv_k_kernel(tc, x, W_words, W_scales, out):
                 )
             if quad == 0:
                 make_identity(nc, ident_f32[:])
-            for g in range(4 * quad, 4 * quad + 4):
+            for g in range(4 * quad, min(4 * quad + 4, FIRST_SPLIT)):
                 words = weights.tile([P, OUT_CH], U32, name="words%d" % g, align_bytes=64)
                 nc.sync.dma_start(
                     out=words[:].bitcast(I32),
                     in_=W_words[g].rearrange("p n t -> p (n t)").bitcast(I32),
                 )
-                w_words.append(words)
+                for half in range(HALVES):
+                    w_cols[(g, half)] = words[:, N_TILE * half : N_TILE * (half + 1)]
+        for half in range(HALVES):
+            for g in range(FIRST_SPLIT, GROUPS):
+                words = weights.tile([P, N_TILE], U32, name="words%d_%d" % (g, half), align_bytes=64)
+                nc.sync.dma_start(
+                    out=words[:].bitcast(I32),
+                    in_=W_words[g, :, N_TILE * half : N_TILE * (half + 1), :]
+                    .rearrange("p n t -> p (n t)")
+                    .bitcast(I32),
+                )
+                w_cols[(g, half)] = words[:]
 
         rows = xs[:].rearrange("p n (r w) -> p n r w", w=SIDE)
         windows = const.tile([P, TAPS // 2, IMAGES, GRID, GRID], BF16)
@@ -98,7 +112,7 @@ def tile_fast2order_de_conv_k_kernel(tc, x, W_words, W_scales, out):
         )
 
         acc = [
-            acc_pool.tile([P, N_TILE], F32, name="acc%d" % half) for half in range(OUT_CH // N_TILE)
+acc_pool.tile([P, N_TILE], F32, name="acc%d" % half) for half in range(HALVES)
         ]
         grouped_of = {}
 
@@ -137,20 +151,20 @@ def tile_fast2order_de_conv_k_kernel(tc, x, W_words, W_scales, out):
                 scales=scales[:],
                 in_=grouped_of[chunk][:].rearrange("p g r t -> p (g r t)"),
             )
-            for g_in_chunk in range(CHUNK):
-                g = CHUNK * chunk + g_in_chunk
-                cols = slice(POSITIONS * g_in_chunk, POSITIONS * (g_in_chunk + 1))
-                for half in range(OUT_CH // N_TILE):
-                    n_cols = slice(N_TILE * half, N_TILE * (half + 1))
-                    nc.tensor.matmul_mx(
-                        out=acc[half][:],
-                        lhsT=codes[:, cols].bitcast(FP8X4),
-                        lhsT_scale=scales[:, cols],
-                        rhs=w_words[g][:, n_cols].bitcast(FP8X4),
-                        rhs_scale=w_planes[g // 4][4 * (g % 4) : P, n_cols],
-                        start=(g == 0),
-                        stop=(g == GROUPS - 1),
-                    )
+            groups = range(CHUNK * chunk, CHUNK * (chunk + 1))
+            whole = [(g, half) for g in groups if g < FIRST_SPLIT for half in range(HALVES)]
+            split = [(g, half) for half in range(HALVES) for g in groups if g >= FIRST_SPLIT]
+            for g, half in whole + split:
+                cols = slice(POSITIONS * (g % CHUNK), POSITIONS * (g % CHUNK + 1))
+                nc.tensor.matmul_mx(
+                    out=acc[half][:],
+                    lhsT=codes[:, cols].bitcast(FP8X4),
+                    lhsT_scale=scales[:, cols],
+                    rhs=w_cols[(g, half)].bitcast(FP8X4),
+                    rhs_scale=w_planes[g // 4][4 * (g % 4) : P, N_TILE * half : N_TILE * (half + 1)],
+                    start=(g == 0),
+                    stop=(g == GROUPS - 1),
+                )
 
         for step in range(CHUNKS + LEAD):
             if step < CHUNKS:
@@ -158,24 +172,26 @@ def tile_fast2order_de_conv_k_kernel(tc, x, W_words, W_scales, out):
             if step >= LEAD:
                 quantise_and_contract(step - LEAD)
 
-        by_position = const.tile([P, OUT_CH], F32)
-        nc.vector.tensor_copy(out=by_position[:, 0:N_TILE], in_=acc[0][:])
-        nc.scalar.copy(out=by_position[:, N_TILE : 2 * N_TILE], in_=acc[1][:])
-        by_channel = const.tile([P, OUT_CH // P, POSITIONS], F32)
-        out_view = out.rearrange("n (t p) y z -> p t n (y z)", p=P)
-        per_bank = N_TILE // P
-        for half in range(OUT_CH // N_TILE):
-            turned_out = turn_pool.tile([P, per_bank, POSITIONS], F32, tag="turn")
-            for t in range(per_bank):
-                o0 = N_TILE * half + P * t
-                nc.tensor.transpose(turned_out[:, t, :], by_position[:, o0 : o0 + P], ident_f32[:])
-            tiles = slice(per_bank * half, per_bank * (half + 1))
+        def leave_psum(half, dst, src):
             if half == 0:
-                nc.vector.tensor_copy(out=by_channel[:, tiles, :], in_=turned_out[:])
+                nc.vector.tensor_copy(out=dst, in_=src)
             else:
-                nc.scalar.copy(out=by_channel[:, tiles, :], in_=turned_out[:])
-            for n in range(IMAGES):
-                nc.sync.dma_start(
-                    out=out_view[:, tiles, n, :],
-                    in_=by_channel[:, tiles, GRID * GRID * n : GRID * GRID * (n + 1)],
-                )
+                nc.scalar.copy(out=dst, in_=src)
+
+        by_position = const.tile([P, HALVES, PER_ROW, P], F32)
+        for half in range(HALVES):
+            leave_psum(half, by_position[:, half], acc[half][:].rearrange("r (p t) -> r t p", t=PER_ROW))
+        by_channel = const.tile([P, HALVES, IMAGES, PER_ROW, GRID * GRID], F32)
+        out_view = out.rearrange("n (h p t) y z -> h p n (t y z)", h=HALVES, t=PER_ROW)
+        for half in range(HALVES):
+            turned_out = turn_pool.tile([P, PER_ROW, POSITIONS], F32, tag="turn")
+            for t in range(PER_ROW):
+                nc.tensor.transpose(turned_out[:, t, :], by_position[:, half, t, :], ident_f32[:])
+            leave_psum(
+                half,
+                by_channel[:, half].rearrange("p n t s -> p t n s"),
+                turned_out[:].rearrange("p t (n s) -> p t n s", n=IMAGES),
+            )
+            nc.sync.dma_start(
+                out=out_view[half], in_=by_channel[:, half].rearrange("p n t s -> p n (t s)")
+            )

@@ -42,7 +42,7 @@ def tile_fast2order_de_conv_k_kernel(tc, x, W_words, W_scales, out):
         turn_pool = ctx.enter_context(tc.psum_pool(name="turn", bufs=6))
         ctx.enter_context(tc.manual_schedule())
 
-        xs = const.tile([P, IMAGES, SIDE * SIDE], BF16)
+        xs = const.tile([P, IMAGES, SIDE * SIDE + 1], BF16)
         x_by_channel = x.rearrange("n c h w -> c n (h w)")
         run = SIDE * SIDE - 1
         for h in range(2):
@@ -87,7 +87,7 @@ def tile_fast2order_de_conv_k_kernel(tc, x, W_words, W_scales, out):
                 )
                 w_cols[(g, half)] = words[:]
 
-        rows = xs[:].rearrange("p n (r w) -> p n r w", w=SIDE)
+        rows = xs[:, :, 0 : SIDE * SIDE].rearrange("p n (r w) -> p n r w", w=SIDE)
         windows = const.tile([P, TAPS // 2, IMAGES, GRID, GRID], BF16)
         for s in range(TAPS // 2):
             a, b_hi = divmod(s, 2)

@@ -21,11 +21,10 @@ GROUPS = CHANNELS * TAPS * TAPS // K_PASS
 CHUNK = 4
 CHUNKS = GROUPS // CHUNK
 CHUNK_CH = 2 * CHUNK
-N_TILE = 512
-HALVES = OUT_CH // N_TILE
+BANK = 512
+PIECES = ((0, 512), (512, 256), (768, 256))
 LEAD = 1
-FIRST_SPLIT = GROUPS - 2
-PER_ROW = N_TILE // P
+FIRST_SPLIT = GROUPS - 3
 
 FLOPS = 2 * POSITIONS * CHANNELS * TAPS * TAPS * OUT_CH
 
@@ -39,7 +38,7 @@ def tile_fast2order_de_conv_k_kernel(tc, x, W_words, W_scales, out):
         feat_pool = ctx.enter_context(tc.tile_pool(name="feat", bufs=3))
         grouped_pool = ctx.enter_context(tc.tile_pool(name="grouped", bufs=3))
         acc_pool = ctx.enter_context(tc.psum_pool(name="acc", bufs=1))
-        turn_pool = ctx.enter_context(tc.psum_pool(name="turn", bufs=6))
+        turn_pool = ctx.enter_context(tc.psum_pool(name="turn", bufs=5))
         ctx.enter_context(tc.manual_schedule())
 
         xs = const.tile([P, IMAGES, SIDE * SIDE + 1], BF16)
@@ -74,18 +73,24 @@ def tile_fast2order_de_conv_k_kernel(tc, x, W_words, W_scales, out):
                     out=words[:].bitcast(I32),
                     in_=W_words[g].rearrange("p n t -> p (n t)").bitcast(I32),
                 )
-                for half in range(HALVES):
-                    w_cols[(g, half)] = words[:, N_TILE * half : N_TILE * (half + 1)]
-        for half in range(HALVES):
-            for g in range(FIRST_SPLIT, GROUPS):
-                words = weights.tile([P, N_TILE], U32, name="words%d_%d" % (g, half), align_bytes=64)
-                nc.sync.dma_start(
-                    out=words[:].bitcast(I32),
-                    in_=W_words[g, :, N_TILE * half : N_TILE * (half + 1), :]
-                    .rearrange("p n t -> p (n t)")
-                    .bitcast(I32),
-                )
-                w_cols[(g, half)] = words[:]
+                for k, (first, width) in enumerate(PIECES):
+                    w_cols[(g, k)] = words[:, first : first + width]
+
+        def load_columns(g, first, width, pieces):
+            words = weights.tile([P, width], U32, name="words%d_%d" % (g, first), align_bytes=64)
+            nc.sync.dma_start(
+                out=words[:].bitcast(I32),
+                in_=W_words[g, :, first : first + width, :].rearrange("p n t -> p (n t)").bitcast(I32),
+            )
+            for k in pieces:
+                w_cols[(g, k)] = words[:, PIECES[k][0] - first : PIECES[k][0] - first + PIECES[k][1]]
+
+        for g in range(FIRST_SPLIT, GROUPS):
+            load_columns(g, 0, 512, (0,))
+        load_columns(FIRST_SPLIT, 512, 512, (1, 2))
+        for k in (1, 2):
+            for g in range(FIRST_SPLIT + 1, GROUPS):
+                load_columns(g, PIECES[k][0], PIECES[k][1], (k,))
 
         rows = xs[:, :, 0 : SIDE * SIDE].rearrange("p n (r w) -> p n r w", w=SIDE)
         windows = const.tile([P, TAPS // 2, IMAGES, GRID, GRID], BF16)
@@ -111,9 +116,7 @@ def tile_fast2order_de_conv_k_kernel(tc, x, W_words, W_scales, out):
             in_=patches[:].bitcast(F32).rearrange("p c (jh u) -> p u c jh", u=2),
         )
 
-        acc = [
-acc_pool.tile([P, N_TILE], F32, name="acc%d" % half) for half in range(HALVES)
-        ]
+        acc = [acc_pool.tile([P, BANK], F32, name="acc%d" % k) for k in range(len(PIECES))]
         grouped_of = {}
 
         def multiply_and_turn(chunk):
@@ -143,7 +146,7 @@ acc_pool.tile([P, N_TILE], F32, name="acc%d" % half) for half in range(HALVES)
                 )
             grouped_of[chunk] = grouped
 
-        def quantise_and_contract(chunk):
+        def quantise(chunk):
             codes = codes_pool.tile([P, CHUNK * POSITIONS], U32, name="codes%d" % chunk, align_bytes=64)
             scales = codes_pool.tile([P, CHUNK * POSITIONS], U8, name="scales%d" % chunk, align_bytes=64)
             nc.vector.quantize_mx(
@@ -151,47 +154,82 @@ acc_pool.tile([P, N_TILE], F32, name="acc%d" % half) for half in range(HALVES)
                 scales=scales[:],
                 in_=grouped_of[chunk][:].rearrange("p g r t -> p (g r t)"),
             )
-            groups = range(CHUNK * chunk, CHUNK * (chunk + 1))
-            whole = [(g, half) for g in groups if g < FIRST_SPLIT for half in range(HALVES)]
-            split = [(g, half) for half in range(HALVES) for g in groups if g >= FIRST_SPLIT]
-            for g, half in whole + split:
-                cols = slice(POSITIONS * (g % CHUNK), POSITIONS * (g % CHUNK + 1))
-                nc.tensor.matmul_mx(
-                    out=acc[half][:],
-                    lhsT=codes[:, cols].bitcast(FP8X4),
-                    lhsT_scale=scales[:, cols],
-                    rhs=w_cols[(g, half)].bitcast(FP8X4),
-                    rhs_scale=w_planes[g // 4][4 * (g % 4) : P, N_TILE * half : N_TILE * (half + 1)],
-                    start=(g == 0),
-                    stop=(g == GROUPS - 1),
-                )
+            return codes, scales
+
+        def contract(operand, g, k):
+            codes, scales = operand
+            first, width = PIECES[k]
+            cols = slice(POSITIONS * (g % CHUNK), POSITIONS * (g % CHUNK + 1))
+            nc.tensor.matmul_mx(
+                out=acc[k][:, 0:width],
+                lhsT=codes[:, cols].bitcast(FP8X4),
+                lhsT_scale=scales[:, cols],
+                rhs=w_cols[(g, k)].bitcast(FP8X4),
+                rhs_scale=w_planes[g // 4][4 * (g % 4) : P, first : first + width],
+                start=(g == 0),
+                stop=(g == GROUPS - 1),
+            )
+
+        by_position = {}
+        by_channel = {}
+        turned_out = {}
+
+        def leave_psum(engine, dst, src):
+            if engine == "vector":
+                nc.vector.tensor_copy(out=dst, in_=src)
+            else:
+                nc.scalar.copy(out=dst, in_=src)
+
+        def sums_to_sbuf(k, engine):
+            width = PIECES[k][1]
+            per_row = width // P
+            by_position[k] = const.tile([P, per_row, P], F32, name="by_position%d" % k)
+            leave_psum(engine, by_position[k][:], acc[k][:, 0:width].rearrange("r (p t) -> r t p", t=per_row))
+
+        def turn_sums(k):
+            per_row = PIECES[k][1] // P
+            turned_out[k] = turn_pool.tile([P, per_row, POSITIONS], F32, tag="turn", name="turned_out%d" % k)
+            for t in range(per_row):
+                nc.tensor.transpose(turned_out[k][:, t, :], by_position[k][:, t, :], ident_f32[:])
+
+        def store(k, engine):
+            first, width = PIECES[k]
+            per_row = width // P
+            by_channel[k] = const.tile([P, IMAGES, per_row, GRID * GRID], F32, name="by_channel%d" % k)
+            leave_psum(
+                engine,
+                by_channel[k][:].rearrange("p n t s -> p t n s"),
+                turned_out[k][:].rearrange("p t (n s) -> p t n s", n=IMAGES),
+            )
+            nc.sync.dma_start(
+                out=out[:, first : first + width].rearrange("n (p t) y z -> p n (t y z)", t=per_row),
+                in_=by_channel[k][:].rearrange("p n t s -> p n (t s)"),
+            )
 
         for step in range(CHUNKS + LEAD):
             if step < CHUNKS:
                 multiply_and_turn(step)
             if step >= LEAD:
-                quantise_and_contract(step - LEAD)
+                chunk = step - LEAD
+                operand = quantise(chunk)
+                for g in range(CHUNK * chunk, min(CHUNK * (chunk + 1), FIRST_SPLIT)):
+                    for k in range(len(PIECES)):
+                        contract(operand, g, k)
 
-        def leave_psum(half, dst, src):
-            if half == 0:
-                nc.vector.tensor_copy(out=dst, in_=src)
-            else:
-                nc.scalar.copy(out=dst, in_=src)
-
-        by_position = const.tile([P, HALVES, PER_ROW, P], F32)
-        for half in range(HALVES):
-            leave_psum(half, by_position[:, half], acc[half][:].rearrange("r (p t) -> r t p", t=PER_ROW))
-        by_channel = const.tile([P, HALVES, IMAGES, PER_ROW, GRID * GRID], F32)
-        out_view = out.rearrange("n (h p t) y z -> h p n (t y z)", h=HALVES, t=PER_ROW)
-        for half in range(HALVES):
-            turned_out = turn_pool.tile([P, PER_ROW, POSITIONS], F32, tag="turn")
-            for t in range(PER_ROW):
-                nc.tensor.transpose(turned_out[:, t, :], by_position[:, half, t, :], ident_f32[:])
-            leave_psum(
-                half,
-                by_channel[:, half].rearrange("p n t s -> p t n s"),
-                turned_out[:].rearrange("p t (n s) -> p t n s", n=IMAGES),
-            )
-            nc.sync.dma_start(
-                out=out_view[half], in_=by_channel[:, half].rearrange("p n t s -> p n (t s)")
-            )
+        for g in range(FIRST_SPLIT, GROUPS):
+            contract(operand, g, 0)
+        sums_to_sbuf(0, "vector")
+        contract(operand, FIRST_SPLIT, 1)
+        contract(operand, FIRST_SPLIT, 2)
+        for g in range(FIRST_SPLIT + 1, GROUPS):
+            contract(operand, g, 1)
+        sums_to_sbuf(1, "scalar")
+        turn_sums(0)
+        for g in range(FIRST_SPLIT + 1, GROUPS):
+            contract(operand, g, 2)
+        sums_to_sbuf(2, "scalar")
+        store(0, "vector")
+        turn_sums(1)
+        store(1, "vector")
+        turn_sums(2)
+        store(2, "scalar")

from contextlib import ExitStack

import concourse.mybir as mybir
from concourse.masks import make_identity

BF16 = mybir.dt.bfloat16
F32 = mybir.dt.float32
I32 = mybir.dt.int32
U32 = mybir.dt.uint32
U8 = mybir.dt.uint8
FP8X4 = mybir.dt.float8_e4m3fn_x4

P = 128
IMAGES, CHANNELS, SIDE = 2, 64, 11
GRID = 8
POSITIONS = IMAGES * GRID * GRID
TAPS = 16
OUT_CH = 1024
K_PASS = 512
GROUPS = CHANNELS * TAPS * TAPS // K_PASS
CHUNK = 4
CHUNKS = GROUPS // CHUNK
CHUNK_CH = 2 * CHUNK
BANK = 512
PIECES = ((0, 512), (512, 256), (768, 256))
LEAD = 1
FIRST_SPLIT = GROUPS - 3

FLOPS = 2 * POSITIONS * CHANNELS * TAPS * TAPS * OUT_CH


def tile_fast2order_de_conv_k_kernel(tc, x, W_words, W_scales, out):
    nc = tc.nc
    with ExitStack() as ctx:
        const = ctx.enter_context(tc.tile_pool(name="const", bufs=1))
        weights = ctx.enter_context(tc.tile_pool(name="weights", bufs=1))
        codes_pool = ctx.enter_context(tc.tile_pool(name="codes", bufs=1))
        feat_pool = ctx.enter_context(tc.tile_pool(name="feat", bufs=3))
        grouped_pool = ctx.enter_context(tc.tile_pool(name="grouped", bufs=3))
        acc_pool = ctx.enter_context(tc.psum_pool(name="acc", bufs=1))
        turn_pool = ctx.enter_context(tc.psum_pool(name="turn", bufs=5))
        ctx.enter_context(tc.manual_schedule())

        xs = const.tile([P, IMAGES, SIDE * SIDE + 1], BF16)
        x_by_channel = x.rearrange("n c h w -> c n (h w)")
        run = SIDE * SIDE - 1
        for h in range(2):
            nc.scalar.dma_start(
                out=xs[CHANNELS * h : CHANNELS * (h + 1), :, 0:run],
                in_=x_by_channel[:, :, h : h + run],
            )

        w_planes = []
        w_cols = {}
        for quad in range(GROUPS // 4):
            planes = weights.tile([P, OUT_CH], U8, name="planes%d" % quad, align_bytes=64)
            nc.vector.memset(planes[:].bitcast(I32), 0)
            w_planes.append(planes)
        ident_bf = const.tile([P, P], BF16)
        make_identity(nc, ident_bf[:])
        ident_f32 = const.tile([P, P], F32)
        for quad in range(GROUPS // 4):
            for q in range(4):
                nc.gpsimd.dma_start(
                    out=w_planes[quad][32 * q : 32 * q + 16, :].bitcast(F32),
                    in_=W_scales[4 * quad : 4 * quad + 4, 4 * q : 4 * q + 4, :].bitcast(F32),
                )
            if quad == 0:
                make_identity(nc, ident_f32[:])
            for g in range(4 * quad, min(4 * quad + 4, FIRST_SPLIT)):
                words = weights.tile([P, OUT_CH], U32, name="words%d" % g, align_bytes=64)
                nc.sync.dma_start(
                    out=words[:].bitcast(I32),
                    in_=W_words[g].rearrange("p n t -> p (n t)").bitcast(I32),
                )
                for k, (first, width) in enumerate(PIECES):
                    w_cols[(g, k)] = words[:, first : first + width]

        def load_columns(g, first, width, pieces):
            words = weights.tile([P, width], U32, name="words%d_%d" % (g, first), align_bytes=64)
            nc.sync.dma_start(
                out=words[:].bitcast(I32),
                in_=W_words[g, :, first : first + width, :].rearrange("p n t -> p (n t)").bitcast(I32),
            )
            for k in pieces:
                w_cols[(g, k)] = words[:, PIECES[k][0] - first : PIECES[k][0] - first + PIECES[k][1]]

        for g in range(FIRST_SPLIT, GROUPS):
            load_columns(g, 0, 512, (0,))
        load_columns(FIRST_SPLIT, 512, 512, (1, 2))
        for k in (1, 2):
            for g in range(FIRST_SPLIT + 1, GROUPS):
                load_columns(g, PIECES[k][0], PIECES[k][1], (k,))

        rows = xs[:, :, 0 : SIDE * SIDE].rearrange("p n (r w) -> p n r w", w=SIDE)
        windows = const.tile([P, TAPS // 2, IMAGES, GRID, GRID], BF16)
        for s in range(TAPS // 2):
            a, b_hi = divmod(s, 2)
            window = rows[:, :, a : a + GRID, 2 * b_hi : 2 * b_hi + GRID]
            if s % 2 == 0:
                nc.vector.tensor_copy(out=windows[:, s], in_=window)
            else:
                nc.scalar.copy(out=windows[:, s], in_=window)
        by_tap = turn_pool.tile([P, TAPS, CHANNELS], BF16, tag="turn")
        for s in range(TAPS // 2):
            nc.tensor.transpose(
                by_tap[:, 2 * s : 2 * s + 2, :].rearrange("p h c -> p (h c)"),
                windows[:, s].rearrange("p n y z -> p (n y z)"),
                ident_bf[:],
            )
        patches = const.tile([P, CHANNELS, TAPS], BF16)
        nc.vector.tensor_copy(out=patches[:], in_=by_tap[:].rearrange("p i c -> p c i"))
        halves = const.tile([P, 2, CHANNELS, TAPS // 2], BF16)
        nc.vector.tensor_copy(
            out=halves[:].bitcast(F32),
            in_=patches[:].bitcast(F32).rearrange("p c (jh u) -> p u c jh", u=2),
        )

        acc = [acc_pool.tile([P, BANK], F32, name="acc%d" % k) for k in range(len(PIECES))]
        grouped_of = {}

        def multiply_and_turn(chunk):
            c0 = CHUNK_CH * chunk
            shape = [P, CHUNK_CH, TAPS, TAPS // 2]
            feat = feat_pool.tile([P, 2, CHUNK_CH, TAPS, TAPS // 2], BF16)
            first = patches[:, c0 : c0 + CHUNK_CH, :].unsqueeze(3).to_broadcast(shape)
            for u in range(2):
                second = halves[:, u, c0 : c0 + CHUNK_CH, :].unsqueeze(2).to_broadcast(shape)
                nc.vector.tensor_mul(out=feat[:, u], in0=first, in1=second)
            feat_words = feat[:].rearrange("p u c i k -> p (u c i k)").bitcast(F32)
            grouped = grouped_pool.tile([P, CHUNK, POSITIONS, 4], BF16, align_bytes=64)
            grouped_words = grouped[:].bitcast(F32)
            for pair in range(CHUNK // 2):
                turned = turn_pool.tile([P, 2, 2, POSITIONS], F32, tag="turn")
                for g_in_pair in range(2):
                    for u in range(2):
                        start = (CHUNK * u + 2 * pair + g_in_pair) * P
                        nc.tensor.transpose(
                            turned[:, g_in_pair, u, :],
                            feat_words[:, start : start + P],
                            ident_f32[:],
                        )
                nc.scalar.copy(
                    out=grouped_words[:, 2 * pair : 2 * pair + 2],
                    in_=turned[:].rearrange("p g u r -> p g r u"),
                )
            grouped_of[chunk] = grouped

        def quantise(chunk):
            codes = codes_pool.tile([P, CHUNK * POSITIONS], U32, name="codes%d" % chunk, align_bytes=64)
            scales = codes_pool.tile([P, CHUNK * POSITIONS], U8, name="scales%d" % chunk, align_bytes=64)
            nc.vector.quantize_mx(
                out=codes[:].bitcast(FP8X4),
                scales=scales[:],
                in_=grouped_of[chunk][:].rearrange("p g r t -> p (g r t)"),
            )
            return codes, scales

        def contract(operand, g, k):
            codes, scales = operand
            first, width = PIECES[k]
            cols = slice(POSITIONS * (g % CHUNK), POSITIONS * (g % CHUNK + 1))
            nc.tensor.matmul_mx(
                out=acc[k][:, 0:width],
                lhsT=codes[:, cols].bitcast(FP8X4),
                lhsT_scale=scales[:, cols],
                rhs=w_cols[(g, k)].bitcast(FP8X4),
                rhs_scale=w_planes[g // 4][4 * (g % 4) : P, first : first + width],
                start=(g == 0),
                stop=(g == GROUPS - 1),
            )

        by_position = {}
        by_channel = {}
        turned_out = {}

        def leave_psum(engine, dst, src):
            if engine == "vector":
                nc.vector.tensor_copy(out=dst, in_=src)
            else:
                nc.scalar.copy(out=dst, in_=src)

        def sums_to_sbuf(k, engine):
            width = PIECES[k][1]
            per_row = width // P
            by_position[k] = const.tile([P, per_row, P], F32, name="by_position%d" % k)
            leave_psum(engine, by_position[k][:], acc[k][:, 0:width].rearrange("r (p t) -> r t p", t=per_row))

        def turn_sums(k):
            per_row = PIECES[k][1] // P
            turned_out[k] = turn_pool.tile([P, per_row, POSITIONS], F32, tag="turn", name="turned_out%d" % k)
            for t in range(per_row):
                nc.tensor.transpose(turned_out[k][:, t, :], by_position[k][:, t, :], ident_f32[:])

        def store(k, engine):
            first, width = PIECES[k]
            per_row = width // P
            by_channel[k] = const.tile([P, IMAGES, per_row, GRID * GRID], F32, name="by_channel%d" % k)
            leave_psum(
                engine,
                by_channel[k][:].rearrange("p n t s -> p t n s"),
                turned_out[k][:].rearrange("p t (n s) -> p t n s", n=IMAGES),
            )
            nc.sync.dma_start(
                out=out[:, first : first + width].rearrange("n (p t) y z -> p n (t y z)", t=per_row),
                in_=by_channel[k][:].rearrange("p n t s -> p n (t s)"),
            )

        for step in range(CHUNKS + LEAD):
            if step < CHUNKS:
                multiply_and_turn(step)
            if step >= LEAD:
                chunk = step - LEAD
                operand = quantise(chunk)
                for g in range(CHUNK * chunk, min(CHUNK * (chunk + 1), FIRST_SPLIT)):
                    for k in range(len(PIECES)):
                        contract(operand, g, k)

        for g in range(FIRST_SPLIT, GROUPS):
            contract(operand, g, 0)
        sums_to_sbuf(0, "vector")
        contract(operand, FIRST_SPLIT, 1)
        contract(operand, FIRST_SPLIT, 2)
        for g in range(FIRST_SPLIT + 1, GROUPS):
            contract(operand, g, 1)
        sums_to_sbuf(1, "scalar")
        turn_sums(0)
        for g in range(FIRST_SPLIT + 1, GROUPS):
            contract(operand, g, 2)
        sums_to_sbuf(2, "scalar")
        store(0, "vector")
        turn_sums(1)
        store(1, "vector")
        turn_sums(2)
        store(2, "scalar")
